import numpy as np
import ml_dtypes


def mxq(x, axis, fmt="e4m3"):
    dtype, down = {"e4m3": (ml_dtypes.float8_e4m3fn, 7), "e5m2": (ml_dtypes.float8_e5m2, 14)}[fmt]
    v = np.moveaxis(np.asarray(x, np.float32).astype(ml_dtypes.bfloat16).astype(np.float64), axis, -1)
    blocks = v.reshape(v.shape[:-1] + (-1, 32))
    amax = np.abs(blocks).max(-1, keepdims=True)
    byte = np.maximum(np.where(amax > 0, np.frexp(amax)[1] - 1 + 127, 0) - down, 1)
    scale = np.exp2(byte - 127.0)
    codes = (blocks / scale).astype(np.float32).astype(dtype).astype(np.float64)
    return np.moveaxis((codes * scale).reshape(v.shape), -1, axis)


WIDE = False


def mx_kscale(k):
    if not WIDE:
        return np.ones(k)
    levels = np.array([10, -10, 5, -5, 0])
    a = np.random.permutation(np.resize(levels, k // 512 * 4)).reshape(k // 512, 4)
    idx = np.arange(k)
    return np.exp2(a[idx // 512, idx % 128 // 32])


BF16 = ml_dtypes.bfloat16


def bf(x):
    return np.asarray(x, np.float32).astype(BF16)


def f64(x):
    return np.asarray(x).astype(np.float64)


NTRAIN, NTEST, D, DY = 512, 8192, 1024, 128
REG = 0.0
EPS = 1e-8
C = 0.5 * np.expm1(2.0 * np.log(NTRAIN / (10.0 * EPS)) / D)


def setup_inputs():
    t = mx_kscale(NTRAIN)
    t = t / np.mean(t)
    ll = bf(0.3 + 0.1 * np.random.standard_normal(1))
    a = np.sqrt(C) * np.exp(f64(ll)[0])
    r = np.sqrt(1.0 - np.log(t) / (0.5 * C * D))
    return {"Ytrain": bf(np.random.standard_normal((NTRAIN, DY)) * 0.15 * np.sqrt(NTRAIN) / t[:, None]),
            "Xtrain": bf(np.random.standard_normal((NTRAIN, D)) * a * r[:, None]),
            "Xtest": bf(np.random.standard_normal((NTEST, D)) * a),
            "log_lengthscale": ll}


def reference(Ytrain, Xtrain, Xtest, log_lengthscale):
    Ytrain, Xtrain, Xtest = f64(Ytrain), f64(Xtrain), f64(Xtest)
    l2 = np.exp(2.0 * f64(log_lengthscale))
    sq = (
        np.sum(Xtest * Xtest, axis=1, keepdims=True)
        + np.sum(Xtrain * Xtrain, axis=1)[None, :]
        - 2.0 * (mxq(Xtest, 1, "e4m3") @ mxq(Xtrain, 1, "e4m3").T)
    )
    K = np.exp(-0.5 * sq / l2) + REG
    numer = mxq(K, 1, "e4m3") @ mxq(Ytrain, 0, "e4m3")
    denom = np.sum(K, axis=1, keepdims=True) + EPS
    return numer / denom

@@ -1,0 +1,233 @@
+import math
+from contextlib import ExitStack
+
+from concourse import mybir
+from concourse.masks import make_identity
+
+F32 = mybir.dt.float32
+BF16 = mybir.dt.bfloat16
+U32 = mybir.dt.uint32
+U8 = mybir.dt.uint8
+I32 = mybir.dt.int32
+FP8X4 = mybir.dt.float8_e4m3fn_x4
+ALU = mybir.AluOpType
+ACT = mybir.ActivationFunctionType
+
+P = 128
+NTRAIN, NTEST, D, DY = 512, 8192, 1024, 128
+EPS = 1e-8
+LN2_HI = 0.693359375
+LN2_LO = math.log(2.0) - LN2_HI
+EXP_DEGREE = 13
+SQ_SCALE = 5033165.0 / 4194304.0
+
+
+def inv_factorial(k):
+    f = 1.0
+    for m in range(2, k + 1):
+        f = f * m
+    return 1.0 / f
+TILES = 4
+CHUNK = P * TILES
+NCHUNK = NTEST // CHUNK
+FLOPS = 2 * NTEST * NTRAIN * D + 2 * NTEST * NTRAIN * DY
+
+
+def tile_nwfunctional_t_kernel(tc, Ytrain, Xtrain, Xtest, log_lengthscale, out):
+    nc = tc.nc
+    with ExitStack() as ctx:
+        const = ctx.enter_context(tc.tile_pool(name="const", bufs=1))
+        xin = ctx.enter_context(tc.tile_pool(name="xin", bufs=NCHUNK))
+        work = ctx.enter_context(tc.tile_pool(name="work", bufs=2))
+        small = ctx.enter_context(tc.tile_pool(name="small", bufs=3))
+        ps_xt = ctx.enter_context(tc.psum_pool(name="ps_xt", bufs=2))
+        ps_s = ctx.enter_context(tc.psum_pool(name="ps_s", bufs=3))
+        ps_kt = ctx.enter_context(tc.psum_pool(name="ps_kt", bufs=2))
+        ps_num = ctx.enter_context(tc.psum_pool(name="ps_num", bufs=1))
+
+        ll = const.tile([P, 1], BF16)
+        nc.sync.dma_start(out=ll[:], in_=log_lengthscale.partition_broadcast(P))
+        xtr = const.tile([P, TILES, D], BF16)
+        nc.sync.dma_start(out=xtr[:], in_=Xtrain.rearrange("(p t) k -> p t k", t=TILES))
+        ynat = const.tile([P, TILES, DY], BF16)
+        nc.sync.dma_start(out=ynat[:], in_=Ytrain.rearrange("(p t) c -> p t c", t=TILES))
+        xs = []
+        for c in range(NCHUNK):
+            xnat = xin.tile([P, TILES, D], BF16, name="xnat")
+            nc.sync.dma_start(
+                out=xnat[:],
+                in_=Xtest[c * CHUNK : (c + 1) * CHUNK, :].rearrange("(p t) k -> p t k", t=TILES),
+            )
+            xs.append(xnat)
+
+        ident_f = const.tile([P, P], F32)
+        make_identity(nc, ident_f[:])
+        ident_b = const.tile([P, P], BF16)
+        make_identity(nc, ident_b[:])
+
+        z = const.tile([P, 1], F32)
+        nc.vector.tensor_scalar_mul(out=z[:], in0=ll[:], scalar1=-2.0)
+        n_raw = const.tile([P, 1], F32)
+        nc.vector.tensor_scalar(
+            out=n_raw[:], in0=z[:], scalar1=1.0 / math.log(2.0), scalar2=126.0, op0=ALU.mult, op1=ALU.min
+        )
+        nc.vector.tensor_scalar_max(out=n_raw[:], in0=n_raw[:], scalar1=-126.0)
+        n_int = const.tile([P, 1], I32)
+        nc.vector.tensor_copy(out=n_int[:], in_=n_raw[:])
+        n_f = const.tile([P, 1], F32)
+        nc.vector.tensor_copy(out=n_f[:], in_=n_int[:])
+        r1 = const.tile([P, 1], F32)
+        nc.vector.scalar_tensor_tensor(
+            out=r1[:], in0=n_f[:], scalar=-LN2_HI, in1=z[:], op0=ALU.mult, op1=ALU.add
+        )
+        r = const.tile([P, 1], F32)
+        nc.vector.scalar_tensor_tensor(
+            out=r[:], in0=n_f[:], scalar=-LN2_LO, in1=r1[:], op0=ALU.mult, op1=ALU.add
+        )
+        acc = const.tile([P, 1], F32)
+        nc.vector.memset(acc[:], inv_factorial(EXP_DEGREE))
+        for k in range(EXP_DEGREE - 1, -1, -1):
+            nc.vector.tensor_scalar(
+                out=acc[:], in0=acc[:], scalar1=r[:, 0:1], scalar2=inv_factorial(k),
+                op0=ALU.mult, op1=ALU.add,
+            )
+        e_int = const.tile([P, 1], I32)
+        nc.vector.tensor_scalar_add(out=e_int[:], in0=n_f[:], scalar1=127.0)
+        p2 = const.tile([P, 1], I32)
+        nc.vector.tensor_single_scalar(out=p2[:], in_=e_int[:], scalar=23, op=ALU.logical_shift_left)
+        s_sb = const.tile([P, 1], F32)
+        nc.vector.tensor_tensor(out=s_sb[:], in0=acc[:], in1=p2[:].bitcast(F32), op=ALU.mult)
+        nhs = const.tile([P, 1], F32)
+        nc.vector.tensor_scalar_mul(out=nhs[:], in0=s_sb[:], scalar1=-0.5 / (SQ_SCALE * SQ_SCALE))
+
+        def sumsq(dst, rows):
+            junk = work.tile([P, D], BF16, name="junk")
+            nc.scalar.activation(out=junk[:], in_=rows, func=ACT.Square, scale=SQ_SCALE, accum_out=dst)
+
+        def transpose_tile(nat, t, grouped_f32):
+            words = nat[:].bitcast(F32)
+            xt = ps_xt.tile([P, 2, 2, P], F32, name="xt")
+            for g in range(2):
+                for u in range(2):
+                    w0 = 256 * g + 128 * u
+                    nc.tensor.transpose(xt[:, g, u, :], words[:, t, w0 : w0 + P], ident_f[:])
+            nc.vector.tensor_copy(out=grouped_f32, in_=xt[:].rearrange("p g u i -> p g i u"))
+
+        sqtr = const.tile([P, TILES], F32)
+        for t in range(TILES):
+            sumsq(sqtr[:, t : t + 1], xtr[:, t, :])
+        ctr = const.tile([P, TILES], F32)
+        nc.vector.tensor_scalar_mul(out=ctr[:], in0=sqtr[:], scalar1=nhs[:, 0:1])
+        rep = const.tile([P, TILES, P], F32)
+        nc.vector.tensor_copy(out=rep[:], in_=ctr[:].unsqueeze(2).to_broadcast([P, TILES, P]))
+        cps = ps_s.tile([P, TILES, P], F32, name="s_ps")
+        for t in range(TILES):
+            nc.tensor.transpose(cps[:, t, :], rep[:, t, :], ident_f[:])
+        c_sb = const.tile([P, NTRAIN], F32)
+        nc.vector.tensor_copy(out=c_sb[:], in_=cps[:].rearrange("p t i -> p (t i)"))
+
+        gtr = const.tile([P, 2, NTRAIN, 4], BF16, align_bytes=64)
+        gtr_f = gtr[:].bitcast(F32)
+        for t in range(TILES):
+            transpose_tile(xtr, t, gtr_f[:, :, t * P : (t + 1) * P, :])
+        tr_codes = const.tile([P, 2, NTRAIN], U32, align_bytes=64)
+        tr_scales = const.tile([P, 2, NTRAIN], U8, align_bytes=64)
+        nc.vector.quantize_mx(
+            out=tr_codes[:].rearrange("p g n -> p (g n)").bitcast(FP8X4),
+            scales=tr_scales[:].rearrange("p g n -> p (g n)"),
+            in_=gtr[:].rearrange("p g n t -> p (g n t)"),
+        )
+
+        ygrp = const.tile([P, DY, 4], BF16, align_bytes=64)
+        nc.vector.tensor_copy(out=ygrp[:], in_=ynat[:].rearrange("p t c -> p c t"))
+        y_codes = const.tile([P, DY], U32, align_bytes=64)
+        y_scales = const.tile([P, DY], U8, align_bytes=64)
+        nc.vector.quantize_mx(
+            out=y_codes[:].bitcast(FP8X4), scales=y_scales[:],
+            in_=ygrp[:].rearrange("p c t -> p (c t)"),
+        )
+
+        for c in range(NCHUNK):
+            xnat = xs[c]
+            sqte = small.tile([P, TILES], F32, name="sqte")
+            for t in range(TILES):
+                sumsq(sqte[:, t : t + 1], xnat[:, t, :])
+            bias = small.tile([P, TILES], F32, name="bias")
+            nc.vector.tensor_scalar_mul(out=bias[:], in0=sqte[:], scalar1=nhs[:, 0:1])
+
+            xg = work.tile([P, TILES, 2, P, 4], BF16, name="xg", align_bytes=64)
+            xg_f = xg[:].bitcast(F32)
+            x_codes = work.tile([P, TILES, 2, P], U32, name="x_codes", align_bytes=64)
+            x_scales = work.tile([P, TILES, 2, P], U8, name="x_scales", align_bytes=64)
+            kg = work.tile([P, TILES, P, 4], BF16, name="kg", align_bytes=64)
+            k_codes = work.tile([P, TILES, P], U32, name="k_codes", align_bytes=64)
+            k_scales = work.tile([P, TILES, P], U8, name="k_scales", align_bytes=64)
+            den = small.tile([P, TILES], F32, name="den")
+            num = ps_num.tile([P, TILES, DY], F32, name="num")
+
+            for h in range(2):
+                pair = slice(2 * h, 2 * h + 2)
+                for t in (2 * h, 2 * h + 1):
+                    transpose_tile(xnat, t, xg_f[:, t])
+                nc.vector.quantize_mx(
+                    out=x_codes[:, pair].rearrange("p a g i -> p (a g i)").bitcast(FP8X4),
+                    scales=x_scales[:, pair].rearrange("p a g i -> p (a g i)"),
+                    in_=xg[:, pair].rearrange("p a g i t -> p (a g i t)"),
+                )
+                kt = ps_kt.tile([P, 2, 4, P], BF16, name="kt")
+                for a in range(2):
+                    t = 2 * h + a
+                    s_ps = ps_s.tile([P, NTRAIN], F32, name="s_ps")
+                    for g in range(2):
+                        nc.tensor.matmul_mx(
+                            out=s_ps[:],
+                            lhsT=x_codes[:, t, g, :].bitcast(FP8X4),
+                            lhsT_scale=x_scales[:, t, g, :],
+                            rhs=tr_codes[:, g, :].bitcast(FP8X4),
+                            rhs_scale=tr_scales[:, g, :],
+                            start=(g == 0),
+                            stop=(g == 1),
+                        )
+                    arg = work.tile([P, NTRAIN], F32, name="arg", bufs=3)
+                    nc.vector.scalar_tensor_tensor(
+                        out=arg[:], in0=s_ps[:], scalar=s_sb[:, 0:1], in1=c_sb[:],
+                        op0=ALU.mult, op1=ALU.add,
+                    )
+                    k_sb = work.tile([P, NTRAIN], BF16, name="k_sb", bufs=3)
+                    nc.scalar.activation(
+                        out=k_sb[:], in_=arg[:], func=ACT.Exp, bias=bias[:, t : t + 1], scale=1.0,
+                        accum_out=den[:, t : t + 1],
+                    )
+                    for q in range(4):
+                        nc.tensor.transpose(kt[:, a, q, :], k_sb[:, q * P : (q + 1) * P], ident_b[:])
+                if h == 0:
+                    nc.scalar.copy(out=kg[:, pair], in_=kt[:].rearrange("p a q i -> p a i q"))
+                else:
+                    nc.vector.tensor_copy(out=kg[:, pair], in_=kt[:].rearrange("p a q i -> p a i q"))
+                nc.vector.quantize_mx(
+                    out=k_codes[:, pair].rearrange("p a i -> p (a i)").bitcast(FP8X4),
+                    scales=k_scales[:, pair].rearrange("p a i -> p (a i)"),
+                    in_=kg[:, pair].rearrange("p a i q -> p (a i q)"),
+                )
+                for t in (2 * h, 2 * h + 1):
+                    nc.tensor.matmul_mx(
+                        out=num[:, t, :],
+                        lhsT=k_codes[:, t, :].bitcast(FP8X4),
+                        lhsT_scale=k_scales[:, t, :],
+                        rhs=y_codes[:].bitcast(FP8X4),
+                        rhs_scale=y_scales[:],
+                        start=True,
+                        stop=True,
+                    )
+            rden = small.tile([P, TILES], F32, name="rden")
+            nc.vector.tensor_scalar_add(out=rden[:], in0=den[:], scalar1=EPS)
+            nc.vector.reciprocal(out=rden[:], in_=rden[:])
+            o_sb = work.tile([P, TILES, DY], F32, name="o_sb")
+            nc.vector.tensor_tensor(
+                out=o_sb[:], in0=num[:], in1=rden[:].unsqueeze(2).to_broadcast([P, TILES, DY]),
+                op=ALU.mult,
+            )
+            nc.sync.dma_start(
+                out=out[c * CHUNK : (c + 1) * CHUNK, :].rearrange("(p t) c -> p t c", t=TILES),
+                in_=o_sb[:],
+            )

@@ -18,7 +18,6 @@ NTRAIN, NTEST, D, DY = 512, 8192, 1024, 128
 EPS = 1e-8
 LN2_HI = 0.693359375
 LN2_LO = math.log(2.0) - LN2_HI
-EXP_DEGREE = 13
 SQ_SCALE = 5033165.0 / 4194304.0
 
 
@@ -30,28 +29,32 @@ def inv_factorial(k):
 TILES = 4
 CHUNK = P * TILES
 NCHUNK = NTEST // CHUNK
+NUNIT = 2 * NCHUNK
+ACT_H = (0, 2, 4, 6)
 FLOPS = 2 * NTEST * NTRAIN * D + 2 * NTEST * NTRAIN * DY
 
 
 def tile_nwfunctional_t_kernel(tc, Ytrain, Xtrain, Xtest, log_lengthscale, out):
     nc = tc.nc
     with ExitStack() as ctx:
+        ctx.enter_context(tc.manual_schedule())
         const = ctx.enter_context(tc.tile_pool(name="const", bufs=1))
         xin = ctx.enter_context(tc.tile_pool(name="xin", bufs=NCHUNK))
         work = ctx.enter_context(tc.tile_pool(name="work", bufs=2))
-        small = ctx.enter_context(tc.tile_pool(name="small", bufs=3))
-        ps_xt = ctx.enter_context(tc.psum_pool(name="ps_xt", bufs=2))
-        ps_s = ctx.enter_context(tc.psum_pool(name="ps_s", bufs=3))
+        deep = ctx.enter_context(tc.tile_pool(name="deep", bufs=4))
+        ps_xt = ctx.enter_context(tc.psum_pool(name="ps_xt", bufs=3))
+        ps_s = ctx.enter_context(tc.psum_pool(name="ps_s", bufs=2))
         ps_kt = ctx.enter_context(tc.psum_pool(name="ps_kt", bufs=2))
         ps_num = ctx.enter_context(tc.psum_pool(name="ps_num", bufs=1))
 
         ll = const.tile([P, 1], BF16)
         nc.sync.dma_start(out=ll[:], in_=log_lengthscale.partition_broadcast(P))
         xtr = const.tile([P, TILES, D], BF16)
-        nc.sync.dma_start(out=xtr[:], in_=Xtrain.rearrange("(p t) k -> p t k", t=TILES))
-        ynat = const.tile([P, TILES, DY], BF16)
-        nc.sync.dma_start(out=ynat[:], in_=Ytrain.rearrange("(p t) c -> p t c", t=TILES))
+        xtr_src = Xtrain.rearrange("(p t) k -> p t k", t=TILES)
+        for t in range(TILES):
+            nc.sync.dma_start(out=xtr[:, t, :], in_=xtr_src[:, t, :])
         xs = []
+        ynat = const.tile([P, TILES, DY], BF16)
         for c in range(NCHUNK):
             xnat = xin.tile([P, TILES, D], BF16, name="xnat")
             nc.sync.dma_start(
@@ -59,6 +62,8 @@ def tile_nwfunctional_t_kernel(tc, Ytrain, Xtrain, Xtest, log_lengthscale, out):
                 in_=Xtest[c * CHUNK : (c + 1) * CHUNK, :].rearrange("(p t) k -> p t k", t=TILES),
             )
             xs.append(xnat)
+            if c == 0:
+                nc.sync.dma_start(out=ynat[:], in_=Ytrain.rearrange("(p t) c -> p t c", t=TILES))
 
         ident_f = const.tile([P, P], F32)
         make_identity(nc, ident_f[:])
@@ -66,70 +71,93 @@ def tile_nwfunctional_t_kernel(tc, Ytrain, Xtrain, Xtest, log_lengthscale, out):
         make_identity(nc, ident_b[:])
 
         z = const.tile([P, 1], F32)
-        nc.vector.tensor_scalar_mul(out=z[:], in0=ll[:], scalar1=-2.0)
         n_raw = const.tile([P, 1], F32)
-        nc.vector.tensor_scalar(
-            out=n_raw[:], in0=z[:], scalar1=1.0 / math.log(2.0), scalar2=126.0, op0=ALU.mult, op1=ALU.min
-        )
-        nc.vector.tensor_scalar_max(out=n_raw[:], in0=n_raw[:], scalar1=-126.0)
         n_int = const.tile([P, 1], I32)
-        nc.vector.tensor_copy(out=n_int[:], in_=n_raw[:])
         n_f = const.tile([P, 1], F32)
-        nc.vector.tensor_copy(out=n_f[:], in_=n_int[:])
         r1 = const.tile([P, 1], F32)
-        nc.vector.scalar_tensor_tensor(
-            out=r1[:], in0=n_f[:], scalar=-LN2_HI, in1=z[:], op0=ALU.mult, op1=ALU.add
-        )
         r = const.tile([P, 1], F32)
-        nc.vector.scalar_tensor_tensor(
-            out=r[:], in0=n_f[:], scalar=-LN2_LO, in1=r1[:], op0=ALU.mult, op1=ALU.add
-        )
-        acc = const.tile([P, 1], F32)
-        nc.vector.memset(acc[:], inv_factorial(EXP_DEGREE))
-        for k in range(EXP_DEGREE - 1, -1, -1):
-            nc.vector.tensor_scalar(
-                out=acc[:], in0=acc[:], scalar1=r[:, 0:1], scalar2=inv_factorial(k),
+        r2 = const.tile([P, 1], F32)
+        r4 = const.tile([P, 1], F32)
+        r8 = const.tile([P, 1], F32)
+        e_int = const.tile([P, 1], I32)
+        p2 = const.tile([P, 1], I32)
+        lv0 = const.tile([P, 8], F32)
+        lv1 = const.tile([P, 4], F32)
+        lv2 = const.tile([P, 2], F32)
+        lv3 = const.tile([P, 1], F32)
+        s_sb = const.tile([P, 1], F32)
+        nhs = const.tile([P, 1], F32)
+
+        def fold(dst, src, power):
+            pairs = src[:].rearrange("p (m two) -> p m two", two=2)
+            nc.vector.scalar_tensor_tensor(
+                out=dst[:], in0=pairs[:, :, 1], scalar=power[:, 0:1], in1=pairs[:, :, 0],
                 op0=ALU.mult, op1=ALU.add,
             )
-        e_int = const.tile([P, 1], I32)
-        nc.vector.tensor_scalar_add(out=e_int[:], in0=n_f[:], scalar1=127.0)
-        p2 = const.tile([P, 1], I32)
-        nc.vector.tensor_single_scalar(out=p2[:], in_=e_int[:], scalar=23, op=ALU.logical_shift_left)
-        s_sb = const.tile([P, 1], F32)
-        nc.vector.tensor_tensor(out=s_sb[:], in0=acc[:], in1=p2[:].bitcast(F32), op=ALU.mult)
-        nhs = const.tile([P, 1], F32)
-        nc.vector.tensor_scalar_mul(out=nhs[:], in0=s_sb[:], scalar1=-0.5 / (SQ_SCALE * SQ_SCALE))
+
+        def scale_step(k):
+            if k == 0:
+                nc.vector.tensor_scalar_mul(out=z[:], in0=ll[:], scalar1=-2.0)
+                nc.vector.tensor_scalar(
+                    out=n_raw[:], in0=z[:], scalar1=1.0 / math.log(2.0), scalar2=126.0,
+                    op0=ALU.mult, op1=ALU.min,
+                )
+                nc.vector.tensor_scalar_max(out=n_int[:], in0=n_raw[:], scalar1=-126.0)
+                nc.vector.tensor_copy(out=n_f[:], in_=n_int[:])
+                nc.vector.scalar_tensor_tensor(
+                    out=r1[:], in0=n_f[:], scalar=-LN2_HI, in1=z[:], op0=ALU.mult, op1=ALU.add
+                )
+                nc.vector.tensor_scalar_add(out=e_int[:], in0=n_f[:], scalar1=127.0)
+                nc.vector.scalar_tensor_tensor(
+                    out=r[:], in0=n_f[:], scalar=-LN2_LO, in1=r1[:], op0=ALU.mult, op1=ALU.add
+                )
+                nc.vector.tensor_single_scalar(out=p2[:], in_=e_int[:], scalar=23, op=ALU.logical_shift_left)
+            elif k == 1:
+                for m in range(7):
+                    nc.vector.tensor_scalar(
+                        out=lv0[:, m : m + 1], in0=r[:], scalar1=inv_factorial(2 * m + 1),
+                        scalar2=inv_factorial(2 * m), op0=ALU.mult, op1=ALU.add,
+                    )
+                nc.vector.tensor_tensor(out=r2[:], in0=r[:], in1=r[:], op=ALU.mult)
+            elif k == 2:
+                fold(lv1, lv0, r2)
+                nc.vector.tensor_tensor(out=r4[:], in0=r2[:], in1=r2[:], op=ALU.mult)
+            elif k == 3:
+                fold(lv2, lv1, r4)
+                nc.vector.tensor_tensor(out=r8[:], in0=r4[:], in1=r4[:], op=ALU.mult)
+            elif k == 4:
+                fold(lv3, lv2, r8)
+            elif k == 5:
+                nc.vector.tensor_tensor(out=s_sb[:], in0=lv3[:], in1=p2[:].bitcast(F32), op=ALU.mult)
+            else:
+                nc.vector.tensor_scalar_mul(out=nhs[:], in0=s_sb[:], scalar1=-0.5 / (SQ_SCALE * SQ_SCALE))
+
+        nc.vector.memset(lv0[:, 7:8], 0.0)
+        scale_step(0)
 
         def sumsq(dst, rows):
             junk = work.tile([P, D], BF16, name="junk")
             nc.scalar.activation(out=junk[:], in_=rows, func=ACT.Square, scale=SQ_SCALE, accum_out=dst)
 
-        def transpose_tile(nat, t, grouped_f32):
+        def transposes_x(nat, t):
             words = nat[:].bitcast(F32)
             xt = ps_xt.tile([P, 2, 2, P], F32, name="xt")
             for g in range(2):
                 for u in range(2):
                     w0 = 256 * g + 128 * u
                     nc.tensor.transpose(xt[:, g, u, :], words[:, t, w0 : w0 + P], ident_f[:])
+            return xt
+
+        def empty_x(xt, grouped_f32):
             nc.vector.tensor_copy(out=grouped_f32, in_=xt[:].rearrange("p g u i -> p g i u"))
 
         sqtr = const.tile([P, TILES], F32)
-        for t in range(TILES):
-            sumsq(sqtr[:, t : t + 1], xtr[:, t, :])
-        ctr = const.tile([P, TILES], F32)
-        nc.vector.tensor_scalar_mul(out=ctr[:], in0=sqtr[:], scalar1=nhs[:, 0:1])
-        rep = const.tile([P, TILES, P], F32)
-        nc.vector.tensor_copy(out=rep[:], in_=ctr[:].unsqueeze(2).to_broadcast([P, TILES, P]))
-        cps = ps_s.tile([P, TILES, P], F32, name="s_ps")
-        for t in range(TILES):
-            nc.tensor.transpose(cps[:, t, :], rep[:, t, :], ident_f[:])
-        c_sb = const.tile([P, NTRAIN], F32)
-        nc.vector.tensor_copy(out=c_sb[:], in_=cps[:].rearrange("p t i -> p (t i)"))
-
         gtr = const.tile([P, 2, NTRAIN, 4], BF16, align_bytes=64)
         gtr_f = gtr[:].bitcast(F32)
         for t in range(TILES):
-            transpose_tile(xtr, t, gtr_f[:, :, t * P : (t + 1) * P, :])
+            sumsq(sqtr[:, t : t + 1], xtr[:, t, :])
+            empty_x(transposes_x(xtr, t), gtr_f[:, :, t * P : (t + 1) * P, :])
+            scale_step(t + 1)
         tr_codes = const.tile([P, 2, NTRAIN], U32, align_bytes=64)
         tr_scales = const.tile([P, 2, NTRAIN], U8, align_bytes=64)
         nc.vector.quantize_mx(
@@ -137,97 +165,213 @@ def tile_nwfunctional_t_kernel(tc, Ytrain, Xtrain, Xtest, log_lengthscale, out):
             scales=tr_scales[:].rearrange("p g n -> p (g n)"),
             in_=gtr[:].rearrange("p g n t -> p (g n t)"),
         )
-
-        ygrp = const.tile([P, DY, 4], BF16, align_bytes=64)
-        nc.vector.tensor_copy(out=ygrp[:], in_=ynat[:].rearrange("p t c -> p c t"))
+        scale_step(5)
         y_codes = const.tile([P, DY], U32, align_bytes=64)
         y_scales = const.tile([P, DY], U8, align_bytes=64)
-        nc.vector.quantize_mx(
-            out=y_codes[:].bitcast(FP8X4), scales=y_scales[:],
-            in_=ygrp[:].rearrange("p c t -> p (c t)"),
-        )
+        ygrp = const.tile([P, DY, 4], BF16, align_bytes=64)
 
-        for c in range(NCHUNK):
-            xnat = xs[c]
-            sqte = small.tile([P, TILES], F32, name="sqte")
+        def y_regroup():
+            nc.vector.tensor_copy(out=ygrp[:], in_=ynat[:].rearrange("p t c -> p c t"))
+
+        def y_quantise():
+            nc.vector.quantize_mx(
+                out=y_codes[:].bitcast(FP8X4), scales=y_scales[:],
+                in_=ygrp[:].rearrange("p c t -> p (c t)"),
+            )
+
+        c_sb = const.tile([P, NTRAIN], F32)
+        rep = const.tile([P, TILES, P], F32)
+        st = {}
+
+        def train_norms_1():
+            ctr = const.tile([P, TILES], F32, name="ctr")
+            nc.vector.tensor_scalar_mul(out=ctr[:], in0=sqtr[:], scalar1=nhs[:, 0:1])
+            nc.vector.tensor_copy(out=rep[:], in_=ctr[:].unsqueeze(2).to_broadcast([P, TILES, P]))
+
+        def train_norms_2():
+            cps = ps_num.tile([P, TILES, P], F32, name="num")
             for t in range(TILES):
-                sumsq(sqte[:, t : t + 1], xnat[:, t, :])
-            bias = small.tile([P, TILES], F32, name="bias")
-            nc.vector.tensor_scalar_mul(out=bias[:], in0=sqte[:], scalar1=nhs[:, 0:1])
+                nc.tensor.transpose(cps[:, t, :], rep[:, t, :], ident_f[:])
+            st["cps"] = cps
 
-            xg = work.tile([P, TILES, 2, P, 4], BF16, name="xg", align_bytes=64)
-            xg_f = xg[:].bitcast(F32)
-            x_codes = work.tile([P, TILES, 2, P], U32, name="x_codes", align_bytes=64)
-            x_scales = work.tile([P, TILES, 2, P], U8, name="x_scales", align_bytes=64)
-            kg = work.tile([P, TILES, P, 4], BF16, name="kg", align_bytes=64)
-            k_codes = work.tile([P, TILES, P], U32, name="k_codes", align_bytes=64)
-            k_scales = work.tile([P, TILES, P], U8, name="k_scales", align_bytes=64)
-            den = small.tile([P, TILES], F32, name="den")
-            num = ps_num.tile([P, TILES, DY], F32, name="num")
+        def train_norms_3():
+            nc.vector.tensor_copy(out=c_sb[:], in_=st["cps"][:].rearrange("p t i -> p (t i)"))
 
-            for h in range(2):
-                pair = slice(2 * h, 2 * h + 2)
-                for t in (2 * h, 2 * h + 1):
-                    transpose_tile(xnat, t, xg_f[:, t])
-                nc.vector.quantize_mx(
-                    out=x_codes[:, pair].rearrange("p a g i -> p (a g i)").bitcast(FP8X4),
-                    scales=x_scales[:, pair].rearrange("p a g i -> p (a g i)"),
-                    in_=xg[:, pair].rearrange("p a g i t -> p (a g i t)"),
+        def ok(u):
+            return 0 <= u < NUNIT
+
+        def stage_a(u, a):
+            st["xt", u, a] = transposes_x(xs[u // 2], 2 * (u % 2) + a)
+
+        def stage_b(u, a):
+            if a == 0:
+                st["xg", u] = work.tile([P, 2, 2, P, 4], BF16, name="xg", align_bytes=64)
+            empty_x(st["xt", u, a], st["xg", u][:].bitcast(F32)[:, a])
+
+        def stage_c(u):
+            x_codes = work.tile([P, 2, 2, P], U32, name="x_codes", align_bytes=64)
+            x_scales = work.tile([P, 2, 2, P], U8, name="x_scales", align_bytes=64)
+            nc.vector.quantize_mx(
+                out=x_codes[:].rearrange("p a g i -> p (a g i)").bitcast(FP8X4),
+                scales=x_scales[:].rearrange("p a g i -> p (a g i)"),
+                in_=st["xg", u][:].rearrange("p a g i t -> p (a g i t)"),
+            )
+            st["xq", u] = (x_codes, x_scales)
+
+        def stage_d(u, a):
+            x_codes, x_scales = st["xq", u]
+            s_ps = ps_s.tile([P, NTRAIN], F32, name="s_ps")
+            for g in range(2):
+                nc.tensor.matmul_mx(
+                    out=s_ps[:],
+                    lhsT=x_codes[:, a, g, :].bitcast(FP8X4),
+                    lhsT_scale=x_scales[:, a, g, :],
+                    rhs=tr_codes[:, g, :].bitcast(FP8X4),
+                    rhs_scale=tr_scales[:, g, :],
+                    start=(g == 0),
+                    stop=(g == 1),
                 )
-                kt = ps_kt.tile([P, 2, 4, P], BF16, name="kt")
-                for a in range(2):
-                    t = 2 * h + a
-                    s_ps = ps_s.tile([P, NTRAIN], F32, name="s_ps")
-                    for g in range(2):
-                        nc.tensor.matmul_mx(
-                            out=s_ps[:],
-                            lhsT=x_codes[:, t, g, :].bitcast(FP8X4),
-                            lhsT_scale=x_scales[:, t, g, :],
-                            rhs=tr_codes[:, g, :].bitcast(FP8X4),
-                            rhs_scale=tr_scales[:, g, :],
-                            start=(g == 0),
-                            stop=(g == 1),
-                        )
-                    arg = work.tile([P, NTRAIN], F32, name="arg", bufs=3)
-                    nc.vector.scalar_tensor_tensor(
-                        out=arg[:], in0=s_ps[:], scalar=s_sb[:, 0:1], in1=c_sb[:],
-                        op0=ALU.mult, op1=ALU.add,
-                    )
-                    k_sb = work.tile([P, NTRAIN], BF16, name="k_sb", bufs=3)
-                    nc.scalar.activation(
-                        out=k_sb[:], in_=arg[:], func=ACT.Exp, bias=bias[:, t : t + 1], scale=1.0,
-                        accum_out=den[:, t : t + 1],
-                    )
-                    for q in range(4):
-                        nc.tensor.transpose(kt[:, a, q, :], k_sb[:, q * P : (q + 1) * P], ident_b[:])
-                if h == 0:
-                    nc.scalar.copy(out=kg[:, pair], in_=kt[:].rearrange("p a q i -> p a i q"))
-                else:
-                    nc.vector.tensor_copy(out=kg[:, pair], in_=kt[:].rearrange("p a q i -> p a i q"))
-                nc.vector.quantize_mx(
-                    out=k_codes[:, pair].rearrange("p a i -> p (a i)").bitcast(FP8X4),
-                    scales=k_scales[:, pair].rearrange("p a i -> p (a i)"),
-                    in_=kg[:, pair].rearrange("p a i q -> p (a i q)"),
-                )
-                for t in (2 * h, 2 * h + 1):
-                    nc.tensor.matmul_mx(
-                        out=num[:, t, :],
-                        lhsT=k_codes[:, t, :].bitcast(FP8X4),
-                        lhsT_scale=k_scales[:, t, :],
-                        rhs=y_codes[:].bitcast(FP8X4),
-                        rhs_scale=y_scales[:],
-                        start=True,
-                        stop=True,
-                    )
-            rden = small.tile([P, TILES], F32, name="rden")
-            nc.vector.tensor_scalar_add(out=rden[:], in0=den[:], scalar1=EPS)
-            nc.vector.reciprocal(out=rden[:], in_=rden[:])
-            o_sb = work.tile([P, TILES, DY], F32, name="o_sb")
+            st["s", u, a] = s_ps
+
+        def stage_e(u, a):
+            arg = deep.tile([P, NTRAIN], F32, name="arg")
+            nc.vector.scalar_tensor_tensor(
+                out=arg[:], in0=st["s", u, a][:], scalar=s_sb[:, 0:1], in1=c_sb[:],
+                op0=ALU.mult, op1=ALU.add,
+            )
+            st["arg", u, a] = arg
+
+        def stage_q(u, a):
+            c, t = u // 2, 2 * (u % 2) + a
+            if t == 0:
+                st["sq", c] = deep.tile([P, TILES], F32, name="sq")
+            sumsq(st["sq", c][:, t : t + 1], xs[c][:, t, :])
+
+        def stage_bias(c):
+            bias = deep.tile([P, TILES], F32, name="bias")
+            nc.vector.tensor_scalar_mul(out=bias[:], in0=st["sq", c][:], scalar1=nhs[:, 0:1])
+            st["bias", c] = bias
+
+        def stage_f(u, a):
+            c, t = u // 2, 2 * (u % 2) + a
+            if t == 0:
+                st["den", c] = deep.tile([P, TILES], F32, name="den")
+            k_sb = deep.tile([P, NTRAIN], BF16, name="k_sb")
+            nc.scalar.activation(
+                out=k_sb[:], in_=st["arg", u, a][:], func=ACT.Exp, bias=st["bias", c][:, t : t + 1],
+                scale=1.0, accum_out=st["den", c][:, t : t + 1],
+            )
+            st["k", u, a] = k_sb
+
+        def stage_g(u, a):
+            if a == 0:
+                st["kt", u] = ps_kt.tile([P, 2, 4, P], BF16, name="kt")
+            for q in range(4):
+                nc.tensor.transpose(st["kt", u][:, a, q, :], st["k", u, a][:, q * P : (q + 1) * P], ident_b[:])
+
+        def stage_h(u):
+            kg = work.tile([P, 2, P, 4], BF16, name="kg", align_bytes=64)
+            src = st["kt", u][:].rearrange("p a q i -> p a i q")
+            if u % 8 in ACT_H:
+                nc.scalar.copy(out=kg[:], in_=src)
+            else:
+                nc.vector.tensor_copy(out=kg[:], in_=src)
+            st["kg", u] = kg
+
+        def stage_i(u):
+            k_codes = work.tile([P, 2, P], U32, name="k_codes", align_bytes=64)
+            k_scales = work.tile([P, 2, P], U8, name="k_scales", align_bytes=64)
+            nc.vector.quantize_mx(
+                out=k_codes[:].rearrange("p a i -> p (a i)").bitcast(FP8X4),
+                scales=k_scales[:].rearrange("p a i -> p (a i)"),
+                in_=st["kg", u][:].rearrange("p a i q -> p (a i q)"),
+            )
+            st["kq", u] = (k_codes, k_scales)
+
+        def stage_j(u, a):
+            c, t = u // 2, 2 * (u % 2) + a
+            if t == 0:
+                st["num", c] = ps_num.tile([P, TILES, DY], F32, name="num")
+            k_codes, k_scales = st["kq", u]
+            nc.tensor.matmul_mx(
+                out=st["num", c][:, t, :],
+                lhsT=k_codes[:, a, :].bitcast(FP8X4),
+                lhsT_scale=k_scales[:, a, :],
+                rhs=y_codes[:].bitcast(FP8X4),
+                rhs_scale=y_scales[:],
+                start=True,
+                stop=True,
+            )
+
+        def stage_r1(c):
+            dpe = deep.tile([P, TILES], F32, name="dpe")
+            nc.vector.tensor_scalar_add(out=dpe[:], in0=st["den", c][:], scalar1=EPS)
+            st["dpe", c] = dpe
+
+        def stage_r2(c):
+            rden = deep.tile([P, TILES], F32, name="rden")
+            nc.vector.reciprocal(out=rden[:], in_=st["dpe", c][:])
+            st["rden", c] = rden
+
+        def stage_k(c):
+            rden = st["rden", c]
+            o_sb = deep.tile([P, TILES, DY], F32, name="o_sb")
             nc.vector.tensor_tensor(
-                out=o_sb[:], in0=num[:], in1=rden[:].unsqueeze(2).to_broadcast([P, TILES, DY]),
+                out=o_sb[:], in0=st["num", c][:], in1=rden[:].unsqueeze(2).to_broadcast([P, TILES, DY]),
                 op=ALU.mult,
             )
             nc.sync.dma_start(
                 out=out[c * CHUNK : (c + 1) * CHUNK, :].rearrange("(p t) c -> p t c", t=TILES),
                 in_=o_sb[:],
             )
+
+        for n in range(-1, NUNIT + 8):
+            for a in range(2):
+                if ok(n):
+                    stage_b(n, a)
+                if n == 0 and a == 0:
+                    scale_step(6)
+            for a in range(2):
+                if ok(n + 1):
+                    stage_a(n + 1, a)
+            if n == 1:
+                train_norms_2()
+                train_norms_3()
+            for a in range(2):
+                if ok(n - 3):
+                    stage_g(n - 3, a)
+            if ok(n - 4):
+                stage_h(n - 4)
+            if ok(n - 1):
+                stage_e(n - 1, 0)
+            if ok(n):
+                stage_c(n)
+            if ok(n - 1):
+                stage_e(n - 1, 1)
+            for a in range(2):
+                if ok(n):
+                    stage_d(n, a)
+            if n % 2 == 1 and ok(n - 7):
+                stage_k((n - 7) // 2)
+            for a in range(2):
+                if ok(n - 5):
+                    stage_j(n - 5, a)
+            for a in range(2):
+                if ok(n + 1):
+                    stage_q(n + 1, a)
+                if ok(n - 2):
+                    stage_f(n - 2, a)
+            if n == 0:
+                train_norms_1()
+            if n == 2:
+                y_regroup()
+            if n % 2 == 0 and ok(n - 4):
+                stage_r1((n - 4) // 2)
+            if ok(n - 4):
+                stage_i(n - 4)
+            if n % 2 == 1 and ok(n - 1):
+                stage_bias((n - 1) // 2)
+            if n % 2 == 1 and ok(n - 5):
+                stage_r2((n - 5) // 2)
+            if n == 3:
+                y_quantise()

@@ -19,6 +19,8 @@ EPS = 1e-8
 LN2_HI = 0.693359375
 LN2_LO = math.log(2.0) - LN2_HI
 SQ_SCALE = 5033165.0 / 4194304.0
+HALF_UNSCALED = 0.5 / (SQ_SCALE * SQ_SCALE)
+GRAM_UNITS = (2, 30)
 
 
 def inv_factorial(k):
@@ -30,7 +32,7 @@ TILES = 4
 CHUNK = P * TILES
 NCHUNK = NTEST // CHUNK
 NUNIT = 2 * NCHUNK
-ACT_H = (0, 2, 4, 6)
+ACT_H = (0, 1, 2, 3, 4, 5, 6, 7)
 FLOPS = 2 * NTEST * NTRAIN * D + 2 * NTEST * NTRAIN * DY
 
 
@@ -42,17 +44,20 @@ def tile_nwfunctional_t_kernel(tc, Ytrain, Xtrain, Xtest, log_lengthscale, out):
         xin = ctx.enter_context(tc.tile_pool(name="xin", bufs=NCHUNK))
         work = ctx.enter_context(tc.tile_pool(name="work", bufs=2))
         deep = ctx.enter_context(tc.tile_pool(name="deep", bufs=4))
-        ps_xt = ctx.enter_context(tc.psum_pool(name="ps_xt", bufs=3))
+        ps_xt = ctx.enter_context(tc.psum_pool(name="ps_xt", bufs=2))
+        ps_g = ctx.enter_context(tc.psum_pool(name="ps_g", bufs=1))
         ps_s = ctx.enter_context(tc.psum_pool(name="ps_s", bufs=2))
         ps_kt = ctx.enter_context(tc.psum_pool(name="ps_kt", bufs=2))
         ps_num = ctx.enter_context(tc.psum_pool(name="ps_num", bufs=1))
 
         ll = const.tile([P, 1], BF16)
         nc.sync.dma_start(out=ll[:], in_=log_lengthscale.partition_broadcast(P))
-        xtr = const.tile([P, TILES, D], BF16)
         xtr_src = Xtrain.rearrange("(p t) k -> p t k", t=TILES)
+        xtr = []
         for t in range(TILES):
-            nc.sync.dma_start(out=xtr[:, t, :], in_=xtr_src[:, t, :])
+            xtr_t = const.tile([P, 1, D], BF16, name="xtr%d" % t)
+            nc.sync.dma_start(out=xtr_t[:], in_=xtr_src[:, t : t + 1, :])
+            xtr.append(xtr_t)
         xs = []
         ynat = const.tile([P, TILES, DY], BF16)
         for c in range(NCHUNK):
@@ -86,7 +91,6 @@ def tile_nwfunctional_t_kernel(tc, Ytrain, Xtrain, Xtest, log_lengthscale, out):
         lv2 = const.tile([P, 2], F32)
         lv3 = const.tile([P, 1], F32)
         s_sb = const.tile([P, 1], F32)
-        nhs = const.tile([P, 1], F32)
 
         def fold(dst, src, power):
             pairs = src[:].rearrange("p (m two) -> p m two", two=2)
@@ -127,10 +131,8 @@ def tile_nwfunctional_t_kernel(tc, Ytrain, Xtrain, Xtest, log_lengthscale, out):
                 nc.vector.tensor_tensor(out=r8[:], in0=r4[:], in1=r4[:], op=ALU.mult)
             elif k == 4:
                 fold(lv3, lv2, r8)
-            elif k == 5:
-                nc.vector.tensor_tensor(out=s_sb[:], in0=lv3[:], in1=p2[:].bitcast(F32), op=ALU.mult)
             else:
-                nc.vector.tensor_scalar_mul(out=nhs[:], in0=s_sb[:], scalar1=-0.5 / (SQ_SCALE * SQ_SCALE))
+                nc.vector.tensor_tensor(out=s_sb[:], in0=lv3[:], in1=p2[:].bitcast(F32), op=ALU.mult)
 
         nc.vector.memset(lv0[:, 7:8], 0.0)
         scale_step(0)
@@ -148,15 +150,18 @@ def tile_nwfunctional_t_kernel(tc, Ytrain, Xtrain, Xtest, log_lengthscale, out):
                     nc.tensor.transpose(xt[:, g, u, :], words[:, t, w0 : w0 + P], ident_f[:])
             return xt
 
-        def empty_x(xt, grouped_f32):
-            nc.vector.tensor_copy(out=grouped_f32, in_=xt[:].rearrange("p g u i -> p g i u"))
+        def empty_x(xt, grouped_f32, on_scalar=False):
+            if on_scalar:
+                nc.scalar.copy(out=grouped_f32, in_=xt[:].rearrange("p g u i -> p g i u"))
+            else:
+                nc.vector.tensor_copy(out=grouped_f32, in_=xt[:].rearrange("p g u i -> p g i u"))
 
         sqtr = const.tile([P, TILES], F32)
         gtr = const.tile([P, 2, NTRAIN, 4], BF16, align_bytes=64)
         gtr_f = gtr[:].bitcast(F32)
         for t in range(TILES):
-            sumsq(sqtr[:, t : t + 1], xtr[:, t, :])
-            empty_x(transposes_x(xtr, t), gtr_f[:, :, t * P : (t + 1) * P, :])
+            sumsq(sqtr[:, t : t + 1], xtr[t][:, 0, :])
+            empty_x(transposes_x(xtr[t], 0), gtr_f[:, :, t * P : (t + 1) * P, :])
             scale_step(t + 1)
         tr_codes = const.tile([P, 2, NTRAIN], U32, align_bytes=64)
         tr_scales = const.tile([P, 2, NTRAIN], U8, align_bytes=64)
@@ -184,9 +189,9 @@ def tile_nwfunctional_t_kernel(tc, Ytrain, Xtrain, Xtest, log_lengthscale, out):
         st = {}
 
         def train_norms_1():
-            ctr = const.tile([P, TILES], F32, name="ctr")
-            nc.vector.tensor_scalar_mul(out=ctr[:], in0=sqtr[:], scalar1=nhs[:, 0:1])
-            nc.vector.tensor_copy(out=rep[:], in_=ctr[:].unsqueeze(2).to_broadcast([P, TILES, P]))
+            htr = const.tile([P, TILES], F32, name="htr")
+            nc.vector.tensor_scalar_mul(out=htr[:], in0=sqtr[:], scalar1=HALF_UNSCALED)
+            nc.vector.tensor_copy(out=rep[:], in_=htr[:].unsqueeze(2).to_broadcast([P, TILES, P]))
 
         def train_norms_2():
             cps = ps_num.tile([P, TILES, P], F32, name="num")
@@ -206,7 +211,7 @@ def tile_nwfunctional_t_kernel(tc, Ytrain, Xtrain, Xtest, log_lengthscale, out):
         def stage_b(u, a):
             if a == 0:
                 st["xg", u] = work.tile([P, 2, 2, P, 4], BF16, name="xg", align_bytes=64)
-            empty_x(st["xt", u, a], st["xg", u][:].bitcast(F32)[:, a])
+            empty_x(st["xt", u, a], st["xg", u][:].bitcast(F32)[:, a], u in (1, 2))
 
         def stage_c(u):
             x_codes = work.tile([P, 2, 2, P], U32, name="x_codes", align_bytes=64)
@@ -236,8 +241,8 @@ def tile_nwfunctional_t_kernel(tc, Ytrain, Xtrain, Xtest, log_lengthscale, out):
         def stage_e(u, a):
             arg = deep.tile([P, NTRAIN], F32, name="arg")
             nc.vector.scalar_tensor_tensor(
-                out=arg[:], in0=st["s", u, a][:], scalar=s_sb[:, 0:1], in1=c_sb[:],
-                op0=ALU.mult, op1=ALU.add,
+                out=arg[:], in0=st["s", u, a][:], scalar=st["h", u, a], in1=c_sb[:],
+                op0=ALU.subtract, op1=ALU.subtract,
             )
             st["arg", u, a] = arg
 
@@ -245,12 +250,40 @@ def tile_nwfunctional_t_kernel(tc, Ytrain, Xtrain, Xtest, log_lengthscale, out):
             c, t = u // 2, 2 * (u % 2) + a
             if t == 0:
                 st["sq", c] = deep.tile([P, TILES], F32, name="sq")
-            sumsq(st["sq", c][:, t : t + 1], xs[c][:, t, :])
+                st["nsq", c] = 0
+            col = st["nsq", c]
+            st["nsq", c] = col + 1
+            st["col", u, a] = col
+            sumsq(st["sq", c][:, col : col + 1], xs[c][:, t, :])
 
-        def stage_bias(c):
-            bias = deep.tile([P, TILES], F32, name="bias")
-            nc.vector.tensor_scalar_mul(out=bias[:], in0=st["sq", c][:], scalar1=nhs[:, 0:1])
-            st["bias", c] = bias
+        def stage_h2(c):
+            cols = st["nsq", c]
+            half = deep.tile([P, TILES], F32, name="half")
+            nc.vector.tensor_scalar_mul(out=half[:, 0:cols], in0=st["sq", c][:, 0:cols], scalar1=HALF_UNSCALED)
+            for u in (2 * c, 2 * c + 1):
+                for a in range(2):
+                    if a == 0 or not gram(u):
+                        col = st["col", u, a]
+                        st["h", u, a] = half[:, col : col + 1]
+
+        def gram(u):
+            return GRAM_UNITS[0] <= u < GRAM_UNITS[1]
+
+        def stage_gm(u):
+            g_ps = ps_g.tile([P, P], F32, name="g_ps")
+            for k in range(8):
+                cols = st["xg", u][:, 1, k // 4, :, k % 4]
+                nc.tensor.matmul(out=g_ps[:], lhsT=cols, rhs=cols, start=(k == 0), stop=(k == 7))
+            st["g", u] = g_ps
+
+        def stage_gd(u):
+            hd = deep.tile([P, 1], F32, name="hd")
+            gj = work.tile([P, P], F32, name="gj")
+            nc.vector.scalar_tensor_tensor(
+                out=gj[:], in0=st["g", u][:], scalar=0.5, in1=ident_f[:], op0=ALU.mult, op1=ALU.mult,
+                accum_out=hd[:],
+            )
+            st["h", u, 1] = hd[:, 0:1]
 
         def stage_f(u, a):
             c, t = u // 2, 2 * (u % 2) + a
@@ -258,8 +291,8 @@ def tile_nwfunctional_t_kernel(tc, Ytrain, Xtrain, Xtest, log_lengthscale, out):
                 st["den", c] = deep.tile([P, TILES], F32, name="den")
             k_sb = deep.tile([P, NTRAIN], BF16, name="k_sb")
             nc.scalar.activation(
-                out=k_sb[:], in_=st["arg", u, a][:], func=ACT.Exp, bias=st["bias", c][:, t : t + 1],
-                scale=1.0, accum_out=st["den", c][:, t : t + 1],
+                out=k_sb[:], in_=st["arg", u, a][:], func=ACT.Exp, scale=s_sb[:, 0:1],
+                accum_out=st["den", c][:, t : t + 1],
             )
             st["k", u, a] = k_sb
 
@@ -272,7 +305,7 @@ def tile_nwfunctional_t_kernel(tc, Ytrain, Xtrain, Xtest, log_lengthscale, out):
         def stage_h(u):
             kg = work.tile([P, 2, P, 4], BF16, name="kg", align_bytes=64)
             src = st["kt", u][:].rearrange("p a q i -> p a i q")
-            if u % 8 in ACT_H:
+            if u % 8 in ACT_H and u != NUNIT - 1:
                 nc.scalar.copy(out=kg[:], in_=src)
             else:
                 nc.vector.tensor_copy(out=kg[:], in_=src)
@@ -325,27 +358,33 @@ def tile_nwfunctional_t_kernel(tc, Ytrain, Xtrain, Xtest, log_lengthscale, out):
                 in_=o_sb[:],
             )
 
+        train_norms_1()
         for n in range(-1, NUNIT + 8):
+            if n % 2 == 1 and ok(n - 1):
+                stage_h2((n - 1) // 2)
             for a in range(2):
                 if ok(n):
                     stage_b(n, a)
-                if n == 0 and a == 0:
-                    scale_step(6)
-            for a in range(2):
-                if ok(n + 1):
-                    stage_a(n + 1, a)
-            if n == 1:
-                train_norms_2()
-                train_norms_3()
+            if ok(n - 1) and gram(n - 1):
+                stage_gd(n - 1)
             for a in range(2):
                 if ok(n - 3):
                     stage_g(n - 3, a)
+            for a in range(2):
+                if ok(n + 1):
+                    stage_a(n + 1, a)
+            if n == 0:
+                train_norms_2()
+            if ok(n) and gram(n):
+                stage_gm(n)
             if ok(n - 4):
                 stage_h(n - 4)
             if ok(n - 1):
                 stage_e(n - 1, 0)
             if ok(n):
                 stage_c(n)
+            if n == 0:
+                train_norms_3()
             if ok(n - 1):
                 stage_e(n - 1, 1)
             for a in range(2):
@@ -357,20 +396,16 @@ def tile_nwfunctional_t_kernel(tc, Ytrain, Xtrain, Xtest, log_lengthscale, out):
                 if ok(n - 5):
                     stage_j(n - 5, a)
             for a in range(2):
-                if ok(n + 1):
+                if ok(n + 1) and (a == 0 or not gram(n + 1)):
                     stage_q(n + 1, a)
                 if ok(n - 2):
                     stage_f(n - 2, a)
-            if n == 0:
-                train_norms_1()
             if n == 2:
                 y_regroup()
             if n % 2 == 0 and ok(n - 4):
                 stage_r1((n - 4) // 2)
             if ok(n - 4):
                 stage_i(n - 4)
-            if n % 2 == 1 and ok(n - 1):
-                stage_bias((n - 1) // 2)
             if n % 2 == 1 and ok(n - 5):
                 stage_r2((n - 5) // 2)
             if n == 3:

@@ -32,7 +32,7 @@ TILES = 4
 CHUNK = P * TILES
 NCHUNK = NTEST // CHUNK
 NUNIT = 2 * NCHUNK
-ACT_H = (0, 1, 2, 3, 4, 5, 6, 7)
+ACT_H = (0, 1, 2, 3, 4, 5, 6)
 FLOPS = 2 * NTEST * NTRAIN * D + 2 * NTEST * NTRAIN * DY
 
 
@@ -267,7 +267,7 @@ def tile_nwfunctional_t_kernel(tc, Ytrain, Xtrain, Xtest, log_lengthscale, out):
                         st["h", u, a] = half[:, col : col + 1]
 
         def gram(u):
-            return GRAM_UNITS[0] <= u < GRAM_UNITS[1]
+            return GRAM_UNITS[0] <= u < GRAM_UNITS[1] and u % 3 != 0
 
         def stage_gm(u):
             g_ps = ps_g.tile([P, P], F32, name="g_ps")

@@ -32,7 +32,7 @@ TILES = 4
 CHUNK = P * TILES
 NCHUNK = NTEST // CHUNK
 NUNIT = 2 * NCHUNK
-ACT_H = (0, 1, 2, 3, 4, 5, 6)
+ACT_H = (0, 1, 2, 3, 4, 5, 6, 7)
 FLOPS = 2 * NTEST * NTRAIN * D + 2 * NTEST * NTRAIN * DY
 
 
@@ -211,7 +211,7 @@ def tile_nwfunctional_t_kernel(tc, Ytrain, Xtrain, Xtest, log_lengthscale, out):
         def stage_b(u, a):
             if a == 0:
                 st["xg", u] = work.tile([P, 2, 2, P, 4], BF16, name="xg", align_bytes=64)
-            empty_x(st["xt", u, a], st["xg", u][:].bitcast(F32)[:, a], u in (1, 2))
+            empty_x(st["xt", u, a], st["xg", u][:].bitcast(F32)[:, a], False)
 
         def stage_c(u):
             x_codes = work.tile([P, 2, 2, P], U32, name="x_codes", align_bytes=64)

@@ -52,14 +52,14 @@ def tile_nwfunctional_t_kernel(tc, Ytrain, Xtrain, Xtest, log_lengthscale, out):
 
         ll = const.tile([P, 1], BF16)
         nc.sync.dma_start(out=ll[:], in_=log_lengthscale.partition_broadcast(P))
-        xtr_src = Xtrain.rearrange("(p t) k -> p t k", t=TILES)
+        xtr_src = Xtrain.rearrange("(t p) k -> p t k", t=TILES)
         xtr = []
         for t in range(TILES):
             xtr_t = const.tile([P, 1, D], BF16, name="xtr%d" % t)
             nc.sync.dma_start(out=xtr_t[:], in_=xtr_src[:, t : t + 1, :])
             xtr.append(xtr_t)
         xs = []
-        ynat = const.tile([P, TILES, DY], BF16)
+        ynat = const.tile([P, 2, 2, DY], BF16)
         for c in range(NCHUNK):
             xnat = xin.tile([P, TILES, D], BF16, name="xnat")
             nc.sync.dma_start(
@@ -68,12 +68,10 @@ def tile_nwfunctional_t_kernel(tc, Ytrain, Xtrain, Xtest, log_lengthscale, out):
             )
             xs.append(xnat)
             if c == 0:
-                nc.sync.dma_start(out=ynat[:], in_=Ytrain.rearrange("(p t) c -> p t c", t=TILES))
+                nc.sync.dma_start(out=ynat[:], in_=Ytrain.rearrange("(u p e) c -> p u e c", u=2, e=2))
 
         ident_f = const.tile([P, P], F32)
         make_identity(nc, ident_f[:])
-        ident_b = const.tile([P, P], BF16)
-        make_identity(nc, ident_b[:])
 
         z = const.tile([P, 1], F32)
         n_raw = const.tile([P, 1], F32)
@@ -176,7 +174,7 @@ def tile_nwfunctional_t_kernel(tc, Ytrain, Xtrain, Xtest, log_lengthscale, out):
         ygrp = const.tile([P, DY, 4], BF16, align_bytes=64)
 
         def y_regroup():
-            nc.vector.tensor_copy(out=ygrp[:], in_=ynat[:].rearrange("p t c -> p c t"))
+            nc.vector.tensor_copy(out=ygrp[:], in_=ynat[:].rearrange("p u e c -> p c (u e)"))
 
         def y_quantise():
             nc.vector.quantize_mx(
@@ -298,17 +296,18 @@ def tile_nwfunctional_t_kernel(tc, Ytrain, Xtrain, Xtest, log_lengthscale, out):
 
         def stage_g(u, a):
             if a == 0:
-                st["kt", u] = ps_kt.tile([P, 2, 4, P], BF16, name="kt")
-            for q in range(4):
-                nc.tensor.transpose(st["kt", u][:, a, q, :], st["k", u, a][:, q * P : (q + 1) * P], ident_b[:])
+                st["kt", u] = ps_kt.tile([P, 2, 2, P], F32, name="kt")
+            words = st["k", u, a][:].bitcast(F32)
+            for w in range(2):
+                nc.tensor.transpose(st["kt", u][:, a, w, :], words[:, w * P : (w + 1) * P], ident_f[:])
 
         def stage_h(u):
             kg = work.tile([P, 2, P, 4], BF16, name="kg", align_bytes=64)
-            src = st["kt", u][:].rearrange("p a q i -> p a i q")
+            src = st["kt", u][:].rearrange("p a w i -> p a i w")
             if u % 8 in ACT_H and u != NUNIT - 1:
-                nc.scalar.copy(out=kg[:], in_=src)
+                nc.scalar.copy(out=kg[:].bitcast(F32), in_=src)
             else:
-                nc.vector.tensor_copy(out=kg[:], in_=src)
+                nc.vector.tensor_copy(out=kg[:].bitcast(F32), in_=src)
             st["kg", u] = kg
 
         def stage_i(u):

@@ -209,7 +209,7 @@ def tile_nwfunctional_t_kernel(tc, Ytrain, Xtrain, Xtest, log_lengthscale, out):
         def stage_b(u, a):
             if a == 0:
                 st["xg", u] = work.tile([P, 2, 2, P, 4], BF16, name="xg", align_bytes=64)
-            empty_x(st["xt", u, a], st["xg", u][:].bitcast(F32)[:, a], False)
+            empty_x(st["xt", u, a], st["xg", u][:].bitcast(F32)[:, a], a == 0 and u % 3 == 1)
 
         def stage_c(u):
             x_codes = work.tile([P, 2, 2, P], U32, name="x_codes", align_bytes=64)
@@ -304,7 +304,7 @@ def tile_nwfunctional_t_kernel(tc, Ytrain, Xtrain, Xtest, log_lengthscale, out):
         def stage_h(u):
             kg = work.tile([P, 2, P, 4], BF16, name="kg", align_bytes=64)
             src = st["kt", u][:].rearrange("p a w i -> p a i w")
-            if u % 8 in ACT_H and u != NUNIT - 1:
+            if u % 8 in ACT_H :
                 nc.scalar.copy(out=kg[:].bitcast(F32), in_=src)
             else:
                 nc.vector.tensor_copy(out=kg[:].bitcast(F32), in_=src)
@@ -361,23 +361,24 @@ def tile_nwfunctional_t_kernel(tc, Ytrain, Xtrain, Xtest, log_lengthscale, out):
         for n in range(-1, NUNIT + 8):
             if n % 2 == 1 and ok(n - 1):
                 stage_h2((n - 1) // 2)
-            for a in range(2):
-                if ok(n):
-                    stage_b(n, a)
+            if ok(n):
+                stage_b(n, 0)
+            if ok(n):
+                stage_b(n, 1)
             if ok(n - 1) and gram(n - 1):
                 stage_gd(n - 1)
-            for a in range(2):
-                if ok(n - 3):
-                    stage_g(n - 3, a)
-            for a in range(2):
-                if ok(n + 1):
-                    stage_a(n + 1, a)
+            if ok(n + 1):
+                stage_a(n + 1, 0)
+            if ok(n + 1):
+                stage_a(n + 1, 1)
             if n == 0:
                 train_norms_2()
             if ok(n) and gram(n):
                 stage_gm(n)
-            if ok(n - 4):
-                stage_h(n - 4)
+            if ok(n - 3):
+                stage_g(n - 3, 0)
+            if ok(n - 3):
+                stage_g(n - 3, 1)
             if ok(n - 1):
                 stage_e(n - 1, 0)
             if ok(n):
@@ -386,19 +387,26 @@ def tile_nwfunctional_t_kernel(tc, Ytrain, Xtrain, Xtest, log_lengthscale, out):
                 train_norms_3()
             if ok(n - 1):
                 stage_e(n - 1, 1)
-            for a in range(2):
-                if ok(n):
-                    stage_d(n, a)
+            if ok(n):
+                stage_d(n, 0)
+            if ok(n):
+                stage_d(n, 1)
             if n % 2 == 1 and ok(n - 7):
                 stage_k((n - 7) // 2)
-            for a in range(2):
-                if ok(n - 5):
-                    stage_j(n - 5, a)
-            for a in range(2):
-                if ok(n + 1) and (a == 0 or not gram(n + 1)):
-                    stage_q(n + 1, a)
-                if ok(n - 2):
-                    stage_f(n - 2, a)
+            if ok(n - 5):
+                stage_j(n - 5, 0)
+            if ok(n - 5):
+                stage_j(n - 5, 1)
+            if ok(n + 1):
+                stage_q(n + 1, 0)
+            if ok(n - 2):
+                stage_f(n - 2, 0)
+            if ok(n - 4):
+                stage_h(n - 4)
+            if ok(n + 1) and not gram(n + 1):
+                stage_q(n + 1, 1)
+            if ok(n - 2):
+                stage_f(n - 2, 1)
             if n == 2:
                 y_regroup()
             if n % 2 == 0 and ok(n - 4):

@@ -183,18 +183,17 @@ def tile_nwfunctional_t_kernel(tc, Ytrain, Xtrain, Xtest, log_lengthscale, out):
             )
 
         c_sb = const.tile([P, NTRAIN], F32)
-        rep = const.tile([P, TILES, P], F32)
         st = {}
 
         def train_norms_1():
             htr = const.tile([P, TILES], F32, name="htr")
             nc.vector.tensor_scalar_mul(out=htr[:], in0=sqtr[:], scalar1=HALF_UNSCALED)
-            nc.vector.tensor_copy(out=rep[:], in_=htr[:].unsqueeze(2).to_broadcast([P, TILES, P]))
+            st["htr"] = htr
 
         def train_norms_2():
             cps = ps_num.tile([P, TILES, P], F32, name="num")
             for t in range(TILES):
-                nc.tensor.transpose(cps[:, t, :], rep[:, t, :], ident_f[:])
+                nc.tensor.transpose(cps[:, t, :], st["htr"][:, t : t + 1].to_broadcast([P, P]), ident_f[:])
             st["cps"] = cps
 
         def train_norms_3():
@@ -367,24 +366,24 @@ def tile_nwfunctional_t_kernel(tc, Ytrain, Xtrain, Xtest, log_lengthscale, out):
                 stage_b(n, 1)
             if ok(n - 1) and gram(n - 1):
                 stage_gd(n - 1)
-            if ok(n + 1):
-                stage_a(n + 1, 0)
-            if ok(n + 1):
-                stage_a(n + 1, 1)
             if n == 0:
                 train_norms_2()
             if ok(n) and gram(n):
                 stage_gm(n)
+            if ok(n + 1):
+                stage_a(n + 1, 0)
+            if ok(n + 1):
+                stage_a(n + 1, 1)
             if ok(n - 3):
                 stage_g(n - 3, 0)
             if ok(n - 3):
                 stage_g(n - 3, 1)
             if ok(n - 1):
                 stage_e(n - 1, 0)
-            if ok(n):
-                stage_c(n)
             if n == 0:
                 train_norms_3()
+            if ok(n):
+                stage_c(n)
             if ok(n - 1):
                 stage_e(n - 1, 1)
             if ok(n):

@@ -92,10 +92,11 @@ def tile_nwfunctional_t_kernel(tc, Ytrain, Xtrain, Xtest, log_lengthscale, out):
 
         def fold(dst, src, power):
             pairs = src[:].rearrange("p (m two) -> p m two", two=2)
-            nc.vector.scalar_tensor_tensor(
-                out=dst[:], in0=pairs[:, :, 1], scalar=power[:, 0:1], in1=pairs[:, :, 0],
-                op0=ALU.mult, op1=ALU.add,
+            n = pairs.shape[1]
+            nc.gpsimd.tensor_tensor(
+                out=dst[:], in0=pairs[:, :, 1], in1=power[:, 0:1].to_broadcast([P, n]), op=ALU.mult
             )
+            nc.gpsimd.tensor_tensor(out=dst[:], in0=dst[:], in1=pairs[:, :, 0], op=ALU.add)
 
         def scale_step(k):
             if k == 0:
@@ -116,23 +117,23 @@ def tile_nwfunctional_t_kernel(tc, Ytrain, Xtrain, Xtest, log_lengthscale, out):
                 nc.vector.tensor_single_scalar(out=p2[:], in_=e_int[:], scalar=23, op=ALU.logical_shift_left)
             elif k == 1:
                 for m in range(7):
-                    nc.vector.tensor_scalar(
+                    nc.gpsimd.tensor_scalar(
                         out=lv0[:, m : m + 1], in0=r[:], scalar1=inv_factorial(2 * m + 1),
                         scalar2=inv_factorial(2 * m), op0=ALU.mult, op1=ALU.add,
                     )
-                nc.vector.tensor_tensor(out=r2[:], in0=r[:], in1=r[:], op=ALU.mult)
+                nc.gpsimd.tensor_tensor(out=r2[:], in0=r[:], in1=r[:], op=ALU.mult)
             elif k == 2:
                 fold(lv1, lv0, r2)
-                nc.vector.tensor_tensor(out=r4[:], in0=r2[:], in1=r2[:], op=ALU.mult)
+                nc.gpsimd.tensor_tensor(out=r4[:], in0=r2[:], in1=r2[:], op=ALU.mult)
             elif k == 3:
                 fold(lv2, lv1, r4)
-                nc.vector.tensor_tensor(out=r8[:], in0=r4[:], in1=r4[:], op=ALU.mult)
+                nc.gpsimd.tensor_tensor(out=r8[:], in0=r4[:], in1=r4[:], op=ALU.mult)
             elif k == 4:
                 fold(lv3, lv2, r8)
             else:
-                nc.vector.tensor_tensor(out=s_sb[:], in0=lv3[:], in1=p2[:].bitcast(F32), op=ALU.mult)
+                nc.gpsimd.tensor_tensor(out=s_sb[:], in0=lv3[:], in1=p2[:].bitcast(F32), op=ALU.mult)
 
-        nc.vector.memset(lv0[:, 7:8], 0.0)
+        nc.gpsimd.memset(lv0[:, 7:8], 0.0)
         scale_step(0)
 
         def sumsq(dst, rows):
@@ -256,7 +257,10 @@ def tile_nwfunctional_t_kernel(tc, Ytrain, Xtrain, Xtest, log_lengthscale, out):
         def stage_h2(c):
             cols = st["nsq", c]
             half = deep.tile([P, TILES], F32, name="half")
-            nc.vector.tensor_scalar_mul(out=half[:, 0:cols], in0=st["sq", c][:, 0:cols], scalar1=HALF_UNSCALED)
+            nc.gpsimd.tensor_scalar(
+                out=half[:, 0:cols], in0=st["sq", c][:, 0:cols], scalar1=HALF_UNSCALED, scalar2=0.0,
+                op0=ALU.mult, op1=ALU.add,
+            )
             for u in (2 * c, 2 * c + 1):
                 for a in range(2):
                     if a == 0 or not gram(u):
@@ -336,7 +340,9 @@ def tile_nwfunctional_t_kernel(tc, Ytrain, Xtrain, Xtest, log_lengthscale, out):
 
         def stage_r1(c):
             dpe = deep.tile([P, TILES], F32, name="dpe")
-            nc.vector.tensor_scalar_add(out=dpe[:], in0=st["den", c][:], scalar1=EPS)
+            nc.gpsimd.tensor_scalar(
+                out=dpe[:], in0=st["den", c][:], scalar1=1.0, scalar2=EPS, op0=ALU.mult, op1=ALU.add
+            )
             st["dpe", c] = dpe
 
         def stage_r2(c):

import math
from contextlib import ExitStack

from concourse import mybir
from concourse.masks import make_identity

F32 = mybir.dt.float32
BF16 = mybir.dt.bfloat16
U32 = mybir.dt.uint32
U8 = mybir.dt.uint8
I32 = mybir.dt.int32
FP8X4 = mybir.dt.float8_e4m3fn_x4
ALU = mybir.AluOpType
ACT = mybir.ActivationFunctionType

P = 128
NTRAIN, NTEST, D, DY = 512, 8192, 1024, 128
EPS = 1e-8
LN2_HI = 0.693359375
LN2_LO = math.log(2.0) - LN2_HI
SQ_SCALE = 5033165.0 / 4194304.0
HALF_UNSCALED = 0.5 / (SQ_SCALE * SQ_SCALE)
GRAM_UNITS = (2, 30)


def inv_factorial(k):
    f = 1.0
    for m in range(2, k + 1):
        f = f * m
    return 1.0 / f
TILES = 4
CHUNK = P * TILES
NCHUNK = NTEST // CHUNK
NUNIT = 2 * NCHUNK
ACT_H = (0, 1, 2, 3, 4, 5, 6, 7)
FLOPS = 2 * NTEST * NTRAIN * D + 2 * NTEST * NTRAIN * DY


def tile_nwfunctional_t_kernel(tc, Ytrain, Xtrain, Xtest, log_lengthscale, out):
    nc = tc.nc
    with ExitStack() as ctx:
        ctx.enter_context(tc.manual_schedule())
        const = ctx.enter_context(tc.tile_pool(name="const", bufs=1))
        xin = ctx.enter_context(tc.tile_pool(name="xin", bufs=NCHUNK))
        work = ctx.enter_context(tc.tile_pool(name="work", bufs=2))
        deep = ctx.enter_context(tc.tile_pool(name="deep", bufs=4))
        ps_xt = ctx.enter_context(tc.psum_pool(name="ps_xt", bufs=2))
        ps_g = ctx.enter_context(tc.psum_pool(name="ps_g", bufs=1))
        ps_s = ctx.enter_context(tc.psum_pool(name="ps_s", bufs=2))
        ps_kt = ctx.enter_context(tc.psum_pool(name="ps_kt", bufs=2))
        ps_num = ctx.enter_context(tc.psum_pool(name="ps_num", bufs=1))

        ll = const.tile([P, 1], BF16)
        nc.sync.dma_start(out=ll[:], in_=log_lengthscale.partition_broadcast(P))
        xtr_src = Xtrain.rearrange("(t p) k -> p t k", t=TILES)
        xtr = []
        for t in range(TILES):
            xtr_t = const.tile([P, 1, D], BF16, name="xtr%d" % t)
            nc.sync.dma_start(out=xtr_t[:], in_=xtr_src[:, t : t + 1, :])
            xtr.append(xtr_t)
        xs = []
        ynat = const.tile([P, 2, 2, DY], BF16)
        for c in range(NCHUNK):
            xnat = xin.tile([P, TILES, D], BF16, name="xnat")
            nc.sync.dma_start(
                out=xnat[:],
                in_=Xtest[c * CHUNK : (c + 1) * CHUNK, :].rearrange("(p t) k -> p t k", t=TILES),
            )
            xs.append(xnat)
            if c == 0:
                nc.sync.dma_start(out=ynat[:], in_=Ytrain.rearrange("(u p e) c -> p u e c", u=2, e=2))

        ident_f = const.tile([P, P], F32)
        make_identity(nc, ident_f[:])

        z = const.tile([P, 1], F32)
        n_raw = const.tile([P, 1], F32)
        n_int = const.tile([P, 1], I32)
        n_f = const.tile([P, 1], F32)
        r1 = const.tile([P, 1], F32)
        r = const.tile([P, 1], F32)
        r2 = const.tile([P, 1], F32)
        r4 = const.tile([P, 1], F32)
        r8 = const.tile([P, 1], F32)
        e_int = const.tile([P, 1], I32)
        p2 = const.tile([P, 1], I32)
        lv0 = const.tile([P, 8], F32)
        lv1 = const.tile([P, 4], F32)
        lv2 = const.tile([P, 2], F32)
        lv3 = const.tile([P, 1], F32)
        s_sb = const.tile([P, 1], F32)

        def fold(dst, src, power):
            pairs = src[:].rearrange("p (m two) -> p m two", two=2)
            n = pairs.shape[1]
            nc.gpsimd.tensor_tensor(
                out=dst[:], in0=pairs[:, :, 1], in1=power[:, 0:1].to_broadcast([P, n]), op=ALU.mult
            )
            nc.gpsimd.tensor_tensor(out=dst[:], in0=dst[:], in1=pairs[:, :, 0], op=ALU.add)

        def scale_step(k):
            if k == 0:
                nc.vector.tensor_scalar_mul(out=z[:], in0=ll[:], scalar1=-2.0)
                nc.vector.tensor_scalar(
                    out=n_raw[:], in0=z[:], scalar1=1.0 / math.log(2.0), scalar2=126.0,
                    op0=ALU.mult, op1=ALU.min,
                )
                nc.vector.tensor_scalar_max(out=n_int[:], in0=n_raw[:], scalar1=-126.0)
                nc.vector.tensor_copy(out=n_f[:], in_=n_int[:])
                nc.vector.scalar_tensor_tensor(
                    out=r1[:], in0=n_f[:], scalar=-LN2_HI, in1=z[:], op0=ALU.mult, op1=ALU.add
                )
                nc.vector.tensor_scalar_add(out=e_int[:], in0=n_f[:], scalar1=127.0)
                nc.vector.scalar_tensor_tensor(
                    out=r[:], in0=n_f[:], scalar=-LN2_LO, in1=r1[:], op0=ALU.mult, op1=ALU.add
                )
                nc.vector.tensor_single_scalar(out=p2[:], in_=e_int[:], scalar=23, op=ALU.logical_shift_left)
            elif k == 1:
                for m in range(7):
                    nc.gpsimd.tensor_scalar(
                        out=lv0[:, m : m + 1], in0=r[:], scalar1=inv_factorial(2 * m + 1),
                        scalar2=inv_factorial(2 * m), op0=ALU.mult, op1=ALU.add,
                    )
                nc.gpsimd.tensor_tensor(out=r2[:], in0=r[:], in1=r[:], op=ALU.mult)
            elif k == 2:
                fold(lv1, lv0, r2)
                nc.gpsimd.tensor_tensor(out=r4[:], in0=r2[:], in1=r2[:], op=ALU.mult)
            elif k == 3:
                fold(lv2, lv1, r4)
                nc.gpsimd.tensor_tensor(out=r8[:], in0=r4[:], in1=r4[:], op=ALU.mult)
            elif k == 4:
                fold(lv3, lv2, r8)
            else:
                nc.gpsimd.tensor_tensor(out=s_sb[:], in0=lv3[:], in1=p2[:].bitcast(F32), op=ALU.mult)

        nc.gpsimd.memset(lv0[:, 7:8], 0.0)
        scale_step(0)

        def sumsq(dst, rows):
            junk = work.tile([P, D], BF16, name="junk")
            nc.scalar.activation(out=junk[:], in_=rows, func=ACT.Square, scale=SQ_SCALE, accum_out=dst)

        def transposes_x(nat, t):
            words = nat[:].bitcast(F32)
            xt = ps_xt.tile([P, 2, 2, P], F32, name="xt")
            for g in range(2):
                for u in range(2):
                    w0 = 256 * g + 128 * u
                    nc.tensor.transpose(xt[:, g, u, :], words[:, t, w0 : w0 + P], ident_f[:])
            return xt

        def empty_x(xt, grouped_f32, on_scalar=False):
            if on_scalar:
                nc.scalar.copy(out=grouped_f32, in_=xt[:].rearrange("p g u i -> p g i u"))
            else:
                nc.vector.tensor_copy(out=grouped_f32, in_=xt[:].rearrange("p g u i -> p g i u"))

        sqtr = const.tile([P, TILES], F32)
        gtr = const.tile([P, 2, NTRAIN, 4], BF16, align_bytes=64)
        gtr_f = gtr[:].bitcast(F32)
        for t in range(TILES):
            sumsq(sqtr[:, t : t + 1], xtr[t][:, 0, :])
            empty_x(transposes_x(xtr[t], 0), gtr_f[:, :, t * P : (t + 1) * P, :])
            scale_step(t + 1)
        tr_codes = const.tile([P, 2, NTRAIN], U32, align_bytes=64)
        tr_scales = const.tile([P, 2, NTRAIN], U8, align_bytes=64)
        nc.vector.quantize_mx(
            out=tr_codes[:].rearrange("p g n -> p (g n)").bitcast(FP8X4),
            scales=tr_scales[:].rearrange("p g n -> p (g n)"),
            in_=gtr[:].rearrange("p g n t -> p (g n t)"),
        )
        scale_step(5)
        y_codes = const.tile([P, DY], U32, align_bytes=64)
        y_scales = const.tile([P, DY], U8, align_bytes=64)
        ygrp = const.tile([P, DY, 4], BF16, align_bytes=64)

        def y_regroup():
            nc.vector.tensor_copy(out=ygrp[:], in_=ynat[:].rearrange("p u e c -> p c (u e)"))

        def y_quantise():
            nc.vector.quantize_mx(
                out=y_codes[:].bitcast(FP8X4), scales=y_scales[:],
                in_=ygrp[:].rearrange("p c t -> p (c t)"),
            )

        c_sb = const.tile([P, NTRAIN], F32)
        st = {}

        def train_norms_1():
            htr = const.tile([P, TILES], F32, name="htr")
            nc.vector.tensor_scalar_mul(out=htr[:], in0=sqtr[:], scalar1=HALF_UNSCALED)
            st["htr"] = htr

        def train_norms_2():
            cps = ps_num.tile([P, TILES, P], F32, name="num")
            for t in range(TILES):
                nc.tensor.transpose(cps[:, t, :], st["htr"][:, t : t + 1].to_broadcast([P, P]), ident_f[:])
            st["cps"] = cps

        def train_norms_3():
            nc.vector.tensor_copy(out=c_sb[:], in_=st["cps"][:].rearrange("p t i -> p (t i)"))

        def ok(u):
            return 0 <= u < NUNIT

        def stage_a(u, a):
            st["xt", u, a] = transposes_x(xs[u // 2], 2 * (u % 2) + a)

        def stage_b(u, a):
            if a == 0:
                st["xg", u] = work.tile([P, 2, 2, P, 4], BF16, name="xg", align_bytes=64)
            empty_x(st["xt", u, a], st["xg", u][:].bitcast(F32)[:, a], a == 0 and u % 3 == 1)

        def stage_c(u):
            x_codes = work.tile([P, 2, 2, P], U32, name="x_codes", align_bytes=64)
            x_scales = work.tile([P, 2, 2, P], U8, name="x_scales", align_bytes=64)
            nc.vector.quantize_mx(
                out=x_codes[:].rearrange("p a g i -> p (a g i)").bitcast(FP8X4),
                scales=x_scales[:].rearrange("p a g i -> p (a g i)"),
                in_=st["xg", u][:].rearrange("p a g i t -> p (a g i t)"),
            )
            st["xq", u] = (x_codes, x_scales)

        def stage_d(u, a):
            x_codes, x_scales = st["xq", u]
            s_ps = ps_s.tile([P, NTRAIN], F32, name="s_ps")
            for g in range(2):
                nc.tensor.matmul_mx(
                    out=s_ps[:],
                    lhsT=x_codes[:, a, g, :].bitcast(FP8X4),
                    lhsT_scale=x_scales[:, a, g, :],
                    rhs=tr_codes[:, g, :].bitcast(FP8X4),
                    rhs_scale=tr_scales[:, g, :],
                    start=(g == 0),
                    stop=(g == 1),
                )
            st["s", u, a] = s_ps

        def stage_e(u, a):
            arg = deep.tile([P, NTRAIN], F32, name="arg")
            nc.vector.scalar_tensor_tensor(
                out=arg[:], in0=st["s", u, a][:], scalar=st["h", u, a], in1=c_sb[:],
                op0=ALU.subtract, op1=ALU.subtract,
            )
            st["arg", u, a] = arg

        def stage_q(u, a):
            c, t = u // 2, 2 * (u % 2) + a
            if t == 0:
                st["sq", c] = deep.tile([P, TILES], F32, name="sq")
                st["nsq", c] = 0
            col = st["nsq", c]
            st["nsq", c] = col + 1
            st["col", u, a] = col
            sumsq(st["sq", c][:, col : col + 1], xs[c][:, t, :])

        def stage_h2(c):
            cols = st["nsq", c]
            half = deep.tile([P, TILES], F32, name="half")
            nc.gpsimd.tensor_scalar(
                out=half[:, 0:cols], in0=st["sq", c][:, 0:cols], scalar1=HALF_UNSCALED, scalar2=0.0,
                op0=ALU.mult, op1=ALU.add,
            )
            for u in (2 * c, 2 * c + 1):
                for a in range(2):
                    if a == 0 or not gram(u):
                        col = st["col", u, a]
                        st["h", u, a] = half[:, col : col + 1]

        def gram(u):
            return GRAM_UNITS[0] <= u < GRAM_UNITS[1] and u % 3 != 0

        def stage_gm(u):
            g_ps = ps_g.tile([P, P], F32, name="g_ps")
            for k in range(8):
                cols = st["xg", u][:, 1, k // 4, :, k % 4]
                nc.tensor.matmul(out=g_ps[:], lhsT=cols, rhs=cols, start=(k == 0), stop=(k == 7))
            st["g", u] = g_ps

        def stage_gd(u):
            hd = deep.tile([P, 1], F32, name="hd")
            gj = work.tile([P, P], F32, name="gj")
            nc.vector.scalar_tensor_tensor(
                out=gj[:], in0=st["g", u][:], scalar=0.5, in1=ident_f[:], op0=ALU.mult, op1=ALU.mult,
                accum_out=hd[:],
            )
            st["h", u, 1] = hd[:, 0:1]

        def stage_f(u, a):
            c, t = u // 2, 2 * (u % 2) + a
            if t == 0:
                st["den", c] = deep.tile([P, TILES], F32, name="den")
            k_sb = deep.tile([P, NTRAIN], BF16, name="k_sb")
            nc.scalar.activation(
                out=k_sb[:], in_=st["arg", u, a][:], func=ACT.Exp, scale=s_sb[:, 0:1],
                accum_out=st["den", c][:, t : t + 1],
            )
            st["k", u, a] = k_sb

        def stage_g(u, a):
            if a == 0:
                st["kt", u] = ps_kt.tile([P, 2, 2, P], F32, name="kt")
            words = st["k", u, a][:].bitcast(F32)
            for w in range(2):
                nc.tensor.transpose(st["kt", u][:, a, w, :], words[:, w * P : (w + 1) * P], ident_f[:])

        def stage_h(u):
            kg = work.tile([P, 2, P, 4], BF16, name="kg", align_bytes=64)
            src = st["kt", u][:].rearrange("p a w i -> p a i w")
            if u % 8 in ACT_H :
                nc.scalar.copy(out=kg[:].bitcast(F32), in_=src)
            else:
                nc.vector.tensor_copy(out=kg[:].bitcast(F32), in_=src)
            st["kg", u] = kg

        def stage_i(u):
            k_codes = work.tile([P, 2, P], U32, name="k_codes", align_bytes=64)
            k_scales = work.tile([P, 2, P], U8, name="k_scales", align_bytes=64)
            nc.vector.quantize_mx(
                out=k_codes[:].rearrange("p a i -> p (a i)").bitcast(FP8X4),
                scales=k_scales[:].rearrange("p a i -> p (a i)"),
                in_=st["kg", u][:].rearrange("p a i q -> p (a i q)"),
            )
            st["kq", u] = (k_codes, k_scales)

        def stage_j(u, a):
            c, t = u // 2, 2 * (u % 2) + a
            if t == 0:
                st["num", c] = ps_num.tile([P, TILES, DY], F32, name="num")
            k_codes, k_scales = st["kq", u]
            nc.tensor.matmul_mx(
                out=st["num", c][:, t, :],
                lhsT=k_codes[:, a, :].bitcast(FP8X4),
                lhsT_scale=k_scales[:, a, :],
                rhs=y_codes[:].bitcast(FP8X4),
                rhs_scale=y_scales[:],
                start=True,
                stop=True,
            )

        def stage_r1(c):
            dpe = deep.tile([P, TILES], F32, name="dpe")
            nc.gpsimd.tensor_scalar(
                out=dpe[:], in0=st["den", c][:], scalar1=1.0, scalar2=EPS, op0=ALU.mult, op1=ALU.add
            )
            st["dpe", c] = dpe

        def stage_r2(c):
            rden = deep.tile([P, TILES], F32, name="rden")
            nc.vector.reciprocal(out=rden[:], in_=st["dpe", c][:])
            st["rden", c] = rden

        def stage_k(c):
            rden = st["rden", c]
            o_sb = deep.tile([P, TILES, DY], F32, name="o_sb")
            nc.vector.tensor_tensor(
                out=o_sb[:], in0=st["num", c][:], in1=rden[:].unsqueeze(2).to_broadcast([P, TILES, DY]),
                op=ALU.mult,
            )
            nc.sync.dma_start(
                out=out[c * CHUNK : (c + 1) * CHUNK, :].rearrange("(p t) c -> p t c", t=TILES),
                in_=o_sb[:],
            )

        train_norms_1()
        for n in range(-1, NUNIT + 8):
            if n % 2 == 1 and ok(n - 1):
                stage_h2((n - 1) // 2)
            if ok(n):
                stage_b(n, 0)
            if ok(n):
                stage_b(n, 1)
            if ok(n - 1) and gram(n - 1):
                stage_gd(n - 1)
            if n == 0:
                train_norms_2()
            if ok(n) and gram(n):
                stage_gm(n)
            if ok(n + 1):
                stage_a(n + 1, 0)
            if ok(n + 1):
                stage_a(n + 1, 1)
            if ok(n - 3):
                stage_g(n - 3, 0)
            if ok(n - 3):
                stage_g(n - 3, 1)
            if ok(n - 1):
                stage_e(n - 1, 0)
            if n == 0:
                train_norms_3()
            if ok(n):
                stage_c(n)
            if ok(n - 1):
                stage_e(n - 1, 1)
            if ok(n):
                stage_d(n, 0)
            if ok(n):
                stage_d(n, 1)
            if n % 2 == 1 and ok(n - 7):
                stage_k((n - 7) // 2)
            if ok(n - 5):
                stage_j(n - 5, 0)
            if ok(n - 5):
                stage_j(n - 5, 1)
            if ok(n + 1):
                stage_q(n + 1, 0)
            if ok(n - 2):
                stage_f(n - 2, 0)
            if ok(n - 4):
                stage_h(n - 4)
            if ok(n + 1) and not gram(n + 1):
                stage_q(n + 1, 1)
            if ok(n - 2):
                stage_f(n - 2, 1)
            if n == 2:
                y_regroup()
            if n % 2 == 0 and ok(n - 4):
                stage_r1((n - 4) // 2)
            if ok(n - 4):
                stage_i(n - 4)
            if n % 2 == 1 and ok(n - 5):
                stage_r2((n - 5) // 2)
            if n == 3:
                y_quantise()
